import numpy as np
import ml_dtypes


def mxq(x, axis, fmt="e4m3"):
    dtype, down = {"e4m3": (ml_dtypes.float8_e4m3fn, 7), "e5m2": (ml_dtypes.float8_e5m2, 14)}[fmt]
    v = np.moveaxis(np.asarray(x, np.float32).astype(ml_dtypes.bfloat16).astype(np.float64), axis, -1)
    blocks = v.reshape(v.shape[:-1] + (-1, 32))
    amax = np.abs(blocks).max(-1, keepdims=True)
    byte = np.maximum(np.where(amax > 0, np.frexp(amax)[1] - 1 + 127, 0) - down, 1)
    scale = np.exp2(byte - 127.0)
    codes = (blocks / scale).astype(np.float32).astype(dtype).astype(np.float64)
    return np.moveaxis((codes * scale).reshape(v.shape), -1, axis)


WIDE = False


def mx_kscale(k):
    if not WIDE:
        return np.ones(k)
    levels = np.array([10, -10, 5, -5, 0])
    a = np.random.permutation(np.resize(levels, k // 512 * 4)).reshape(k // 512, 4)
    idx = np.arange(k)
    return np.exp2(a[idx // 512, idx % 128 // 32])


BF16 = ml_dtypes.bfloat16


def bf(x):
    return np.asarray(x, np.float32).astype(BF16)


def f64(x):
    return np.asarray(x).astype(np.float64)


B, HH, WW, C, NH, KD, WS, SS = 1, 32, 32, 256, 8, 64, 8, 4
GH, GW, T, F = HH // WS, WW // WS, WS * WS, NH * KD
N = B * GH * GW


def setup_inputs():
    s = mx_kscale(F).reshape(NH, KD)
    return {"attn_ctx": bf(np.random.standard_normal((N, T, NH, KD)) * 0.4 * s),
            "x": bf(np.random.standard_normal((B, HH, WW, C))),
            "wo": bf(np.random.standard_normal((NH, KD, C)) * 2.0 / np.sqrt(F) / s[:, :, None]),
            "bo": bf(np.random.standard_normal(C) * 0.3)}


def reference(attn_ctx, x, wo, bo):
    o = f64(attn_ctx).reshape(N * T, F)
    proj = (mxq(o, 1, "e4m3") @ mxq(f64(wo).reshape(F, C), 0, "e4m3")) + f64(bo)
    merged = proj.reshape(B, GH, GW, WS, WS, C).swapaxes(2, 3).reshape(B, HH, WW, C)
    merged = np.roll(merged, shift=(SS, SS), axis=(1, 2))
    return f64(x) + merged

@@ -1,0 +1,144 @@
+from contextlib import ExitStack
+
+import concourse.mybir as mybir
+from concourse.masks import make_identity
+
+F32 = mybir.dt.float32
+BF16 = mybir.dt.bfloat16
+U32 = mybir.dt.uint32
+U8 = mybir.dt.uint8
+FP8X4 = mybir.dt.float8_e4m3fn_x4
+ADD = mybir.AluOpType.add
+
+P = 128
+K = 512
+PACK = 4
+HALVES = 2
+C = 256
+SLOTS = 8
+PAIR = 2
+SHIFT = 4
+
+FLOPS = 2 * 1024 * K * C
+
+
+def build_permutations(nc, consts):
+    ident = consts.tile([P, P], F32)
+    make_identity(nc, ident[:])
+    perm_stay = consts.tile([P, P], F32)
+    perm_next = consts.tile([P, P], F32)
+
+    by_token = ident[:].rearrange("p (gi gj th tl) -> p gi th tl gj", gi=4, gj=4, th=2, tl=4)
+    by_pixel = perm_stay[:].rearrange("p (rh rl tl jb) -> p rh rl tl jb", rh=4, rl=2, tl=4, jb=4)
+    nc.vector.tensor_copy(out=by_pixel[:, :, 1], in_=by_token[:, :, 0])
+    nc.vector.tensor_copy(out=by_pixel[:, 1:4, 0], in_=by_token[:, 0:3, 1])
+    nc.vector.tensor_copy(out=by_pixel[:, 0:1, 0], in_=by_token[:, 3:4, 1])
+
+    stay = perm_stay[:].rearrange("p (i jb) -> p i jb", jb=4)
+    moved = perm_next[:].rearrange("p (i jb) -> p i jb", jb=4)
+    nc.vector.tensor_copy(out=moved[:, :, 1:4], in_=stay[:, :, 0:3])
+    nc.vector.tensor_copy(out=moved[:, :, 0:1], in_=stay[:, :, 3:4])
+    return perm_stay, perm_next
+
+
+def tile_windowattentionblock_pb_s_kernel(tc, attn_ctx, x, wo, bo, out):
+    nc = tc.nc
+    with ExitStack() as stack:
+        consts = stack.enter_context(tc.tile_pool(name="consts", bufs=1))
+        work = stack.enter_context(tc.tile_pool(name="work", bufs=SLOTS // PAIR))
+        psum_bias = stack.enter_context(tc.psum_pool(name="psum_bias", bufs=1))
+        psum_t = stack.enter_context(tc.psum_pool(name="psum_t", bufs=3))
+        psum_acc = stack.enter_context(tc.psum_pool(name="psum_acc", bufs=4))
+
+        attn_rows = attn_ctx.rearrange("n (ti tj) h d -> (n ti) (tj h d)", tj=SLOTS)
+        x_rows = x.rearrange("b i (jb s) c -> (b i jb) s c", s=SLOTS)
+        out_rows = out.rearrange("b i (jb s) c -> (b i jb) s c", s=SLOTS)
+        wo_rows = wo.rearrange("h d c -> (h d) c").rearrange(
+            "(u p e) c -> p u (e c)", u=HALVES, p=P
+        )
+
+        perm_stay, perm_next = build_permutations(nc, consts)
+        ones = consts.tile([P, P], BF16)
+        nc.vector.memset(ones[:], 1.0)
+        bo_row0 = consts.tile([P, C], BF16)
+        nc.vector.memset(bo_row0[:], 0.0)
+
+        nc.scalar.dma_start(out=bo_row0[0:1, :], in_=bo.rearrange("(o c) -> o c", o=1))
+        w_raw = consts.tile([P, PACK, C], BF16)
+        nc.sync.dma_start(out=w_raw[:].rearrange("p (u e) c -> p u (e c)", u=HALVES), in_=wo_rows)
+        x_sb = consts.tile([P, SLOTS, C], BF16)
+        for half in range(2):
+            slots = slice(half * SLOTS // 2, (half + 1) * SLOTS // 2)
+            nc.sync.dma_start(out=x_sb[:, slots, :], in_=x_rows[:, slots, :])
+        a_sb = consts.tile([P, SLOTS * K], BF16)
+        for slot in range(0, SLOTS, PAIR):
+            tj = (slot + SHIFT) % SLOTS
+            nc.sync.dma_start(
+                out=a_sb[:, tj * K : (tj + PAIR) * K], in_=attn_rows[:, tj * K : (tj + PAIR) * K]
+            )
+
+        w_grouped = consts.tile([P, C, PACK], BF16, align_bytes=64)
+        nc.scalar.copy(out=w_grouped[:], in_=w_raw[:].rearrange("p t c -> p c t"))
+        w_codes = consts.tile([P, C], U32, align_bytes=64)
+        w_scales = consts.tile([P, C], U8, align_bytes=64)
+        nc.vector.quantize_mx(
+            out=w_codes[:].bitcast(FP8X4),
+            scales=w_scales[:],
+            in_=w_grouped[:].rearrange("p c t -> p (c t)"),
+        )
+
+        bo_all = psum_bias.tile([P, C], F32)
+        nc.tensor.matmul(out=bo_all[:], lhsT=ones[:], rhs=bo_row0[:], start=True, stop=True)
+
+        x_plus_bo = consts.tile([P, SLOTS, C], F32)
+        for slot in range(0, SLOTS, PAIR):
+            nc.vector.tensor_tensor(
+                out=x_plus_bo[:, slot : slot + PAIR, :],
+                in0=x_sb[:, slot : slot + PAIR, :],
+                in1=bo_all[:].unsqueeze(1).to_broadcast([P, PAIR, C]),
+                op=ADD,
+            )
+
+        a_words = a_sb[:].bitcast(F32)
+        words = K // 2
+        for slot in range(0, SLOTS, PAIR):
+            tj = (slot + SHIFT) % SLOTS
+            perm = perm_stay if tj < SHIFT else perm_next
+
+            transposed = psum_t.tile([P, PAIR, HALVES, P], F32)
+            for s in range(PAIR):
+                for u in range(HALVES):
+                    first = (tj + s) * words + u * P
+                    nc.tensor.transpose(
+                        transposed[:, s, u, :], a_words[:, first : first + P], perm[:]
+                    )
+
+            grouped = work.tile([P, PAIR * P * PACK], BF16, align_bytes=64)
+            nc.scalar.copy(
+                out=grouped[:].bitcast(F32).rearrange("p (s q u) -> p s q u", s=PAIR, u=HALVES),
+                in_=transposed[:].rearrange("p s u q -> p s q u"),
+            )
+            a_codes = work.tile([P, PAIR * P], U32, align_bytes=64)
+            a_scales = work.tile([P, PAIR * P], U8, align_bytes=64)
+            nc.vector.quantize_mx(
+                out=a_codes[:].bitcast(FP8X4), scales=a_scales[:], in_=grouped[:]
+            )
+
+            acc = psum_acc.tile([P, PAIR, C], F32)
+            for s in range(PAIR):
+                pixels = slice(s * P, (s + 1) * P)
+                nc.tensor.matmul_mx(
+                    out=acc[:, s, :],
+                    lhsT=a_codes[:, pixels].bitcast(FP8X4),
+                    lhsT_scale=a_scales[:, pixels],
+                    rhs=w_codes[:].bitcast(FP8X4),
+                    rhs_scale=w_scales[:],
+                    start=True,
+                    stop=True,
+                )
+
+            result = work.tile([P, PAIR, C], F32)
+            nc.vector.tensor_tensor(
+                out=result[:], in0=acc[:], in1=x_plus_bo[:, slot : slot + PAIR, :], op=ADD
+            )
+            nc.sync.dma_start(out=out_rows[:, slot : slot + PAIR, :], in_=result[:])

@@ -43,12 +43,14 @@ def build_permutations(nc, consts):
 
 def tile_windowattentionblock_pb_s_kernel(tc, attn_ctx, x, wo, bo, out):
     nc = tc.nc
+    groups = range(SLOTS // PAIR)
     with ExitStack() as stack:
         consts = stack.enter_context(tc.tile_pool(name="consts", bufs=1))
-        work = stack.enter_context(tc.tile_pool(name="work", bufs=SLOTS // PAIR))
+        work = stack.enter_context(tc.tile_pool(name="work", bufs=len(groups)))
         psum_bias = stack.enter_context(tc.psum_pool(name="psum_bias", bufs=1))
-        psum_t = stack.enter_context(tc.psum_pool(name="psum_t", bufs=3))
-        psum_acc = stack.enter_context(tc.psum_pool(name="psum_acc", bufs=4))
+        psum_t = stack.enter_context(tc.psum_pool(name="psum_t", bufs=len(groups)))
+        psum_acc = stack.enter_context(tc.psum_pool(name="psum_acc", bufs=3))
+        stack.enter_context(tc.manual_schedule())
 
         attn_rows = attn_ctx.rearrange("n (ti tj) h d -> (n ti) (tj h d)", tj=SLOTS)
         x_rows = x.rearrange("b i (jb s) c -> (b i jb) s c", s=SLOTS)
@@ -57,13 +59,15 @@ def tile_windowattentionblock_pb_s_kernel(tc, attn_ctx, x, wo, bo, out):
             "(u p e) c -> p u (e c)", u=HALVES, p=P
         )
 
-        perm_stay, perm_next = build_permutations(nc, consts)
-        ones = consts.tile([P, P], BF16)
-        nc.vector.memset(ones[:], 1.0)
+        def slots_of(g):
+            return slice(g * PAIR, (g + 1) * PAIR)
+
+        def first_tj(g):
+            return (g * PAIR + SHIFT) % SLOTS
+
         bo_row0 = consts.tile([P, C], BF16)
         nc.vector.memset(bo_row0[:], 0.0)
-
-        nc.scalar.dma_start(out=bo_row0[0:1, :], in_=bo.rearrange("(o c) -> o c", o=1))
+        nc.sync.dma_start(out=bo_row0[0:1, :], in_=bo.rearrange("(o c) -> o c", o=1))
         w_raw = consts.tile([P, PACK, C], BF16)
         nc.sync.dma_start(out=w_raw[:].rearrange("p (u e) c -> p u (e c)", u=HALVES), in_=wo_rows)
         x_sb = consts.tile([P, SLOTS, C], BF16)
@@ -71,59 +75,74 @@ def tile_windowattentionblock_pb_s_kernel(tc, attn_ctx, x, wo, bo, out):
             slots = slice(half * SLOTS // 2, (half + 1) * SLOTS // 2)
             nc.sync.dma_start(out=x_sb[:, slots, :], in_=x_rows[:, slots, :])
         a_sb = consts.tile([P, SLOTS * K], BF16)
-        for slot in range(0, SLOTS, PAIR):
-            tj = (slot + SHIFT) % SLOTS
-            nc.sync.dma_start(
-                out=a_sb[:, tj * K : (tj + PAIR) * K], in_=attn_rows[:, tj * K : (tj + PAIR) * K]
-            )
+        for g in groups:
+            columns = slice(first_tj(g) * K, (first_tj(g) + PAIR) * K)
+            nc.sync.dma_start(out=a_sb[:, columns], in_=attn_rows[:, columns])
+
+        ones = consts.tile([P, P], BF16)
+        nc.vector.memset(ones[:], 1.0)
+        perm_stay, perm_next = build_permutations(nc, consts)
+
+        bo_all = psum_bias.tile([P, C], F32)
+        nc.tensor.matmul(out=bo_all[:], lhsT=ones[:], rhs=bo_row0[:], start=True, stop=True)
 
         w_grouped = consts.tile([P, C, PACK], BF16, align_bytes=64)
         nc.scalar.copy(out=w_grouped[:], in_=w_raw[:].rearrange("p t c -> p c t"))
         w_codes = consts.tile([P, C], U32, align_bytes=64)
         w_scales = consts.tile([P, C], U8, align_bytes=64)
-        nc.vector.quantize_mx(
-            out=w_codes[:].bitcast(FP8X4),
-            scales=w_scales[:],
-            in_=w_grouped[:].rearrange("p c t -> p (c t)"),
-        )
 
-        bo_all = psum_bias.tile([P, C], F32)
-        nc.tensor.matmul(out=bo_all[:], lhsT=ones[:], rhs=bo_row0[:], start=True, stop=True)
+        def quantise_wo():
+            nc.vector.quantize_mx(
+                out=w_codes[:].bitcast(FP8X4),
+                scales=w_scales[:],
+                in_=w_grouped[:].rearrange("p c t -> p (c t)"),
+            )
 
         x_plus_bo = consts.tile([P, SLOTS, C], F32)
-        for slot in range(0, SLOTS, PAIR):
+
+        def add_bias_to_x(g):
             nc.vector.tensor_tensor(
-                out=x_plus_bo[:, slot : slot + PAIR, :],
-                in0=x_sb[:, slot : slot + PAIR, :],
+                out=x_plus_bo[:, slots_of(g), :],
+                in0=x_sb[:, slots_of(g), :],
                 in1=bo_all[:].unsqueeze(1).to_broadcast([P, PAIR, C]),
                 op=ADD,
             )
 
+        add_bias_to_x(0)
+        add_bias_to_x(1)
+        quantise_wo()
+        add_bias_to_x(2)
+        add_bias_to_x(3)
+
         a_words = a_sb[:].bitcast(F32)
         words = K // 2
-        for slot in range(0, SLOTS, PAIR):
-            tj = (slot + SHIFT) % SLOTS
-            perm = perm_stay if tj < SHIFT else perm_next
-
+        grouped = []
+        for g in groups:
+            perm = perm_stay if first_tj(g) < SHIFT else perm_next
             transposed = psum_t.tile([P, PAIR, HALVES, P], F32)
             for s in range(PAIR):
                 for u in range(HALVES):
-                    first = (tj + s) * words + u * P
+                    first = (first_tj(g) + s) * words + u * P
                     nc.tensor.transpose(
                         transposed[:, s, u, :], a_words[:, first : first + P], perm[:]
                     )
-
-            grouped = work.tile([P, PAIR * P * PACK], BF16, align_bytes=64)
+            side_by_side = work.tile([P, PAIR * P * PACK], BF16, align_bytes=64)
             nc.scalar.copy(
-                out=grouped[:].bitcast(F32).rearrange("p (s q u) -> p s q u", s=PAIR, u=HALVES),
+                out=side_by_side[:]
+                .bitcast(F32)
+                .rearrange("p (s q u) -> p s q u", s=PAIR, u=HALVES),
                 in_=transposed[:].rearrange("p s u q -> p s q u"),
             )
+            grouped.append(side_by_side)
+
+        sums = []
+
+        def project(g):
             a_codes = work.tile([P, PAIR * P], U32, align_bytes=64)
             a_scales = work.tile([P, PAIR * P], U8, align_bytes=64)
             nc.vector.quantize_mx(
-                out=a_codes[:].bitcast(FP8X4), scales=a_scales[:], in_=grouped[:]
+                out=a_codes[:].bitcast(FP8X4), scales=a_scales[:], in_=grouped[g][:]
             )
-
             acc = psum_acc.tile([P, PAIR, C], F32)
             for s in range(PAIR):
                 pixels = slice(s * P, (s + 1) * P)
@@ -136,9 +155,17 @@ def tile_windowattentionblock_pb_s_kernel(tc, attn_ctx, x, wo, bo, out):
                     start=True,
                     stop=True,
                 )
+            sums.append(acc)
 
+        def finish(g):
             result = work.tile([P, PAIR, C], F32)
             nc.vector.tensor_tensor(
-                out=result[:], in0=acc[:], in1=x_plus_bo[:, slot : slot + PAIR, :], op=ADD
+                out=result[:], in0=sums[g][:], in1=x_plus_bo[:, slots_of(g), :], op=ADD
             )
-            nc.sync.dma_start(out=out_rows[:, slot : slot + PAIR, :], in_=result[:])
+            nc.sync.dma_start(out=out_rows[:, slots_of(g), :], in_=result[:])
+
+        project(0)
+        for g in groups[1:]:
+            project(g)
+            finish(g - 1)
+        finish(groups[-1])

@@ -67,12 +67,12 @@ def tile_windowattentionblock_pb_s_kernel(tc, attn_ctx, x, wo, bo, out):
 
         bo_row0 = consts.tile([P, C], BF16)
         nc.vector.memset(bo_row0[:], 0.0)
-        nc.sync.dma_start(out=bo_row0[0:1, :], in_=bo.rearrange("(o c) -> o c", o=1))
         w_raw = consts.tile([P, PACK, C], BF16)
         nc.sync.dma_start(out=w_raw[:].rearrange("p (u e) c -> p u (e c)", u=HALVES), in_=wo_rows)
+        nc.sync.dma_start(out=bo_row0[0:1, :], in_=bo.rearrange("(o c) -> o c", o=1))
         x_sb = consts.tile([P, SLOTS, C], BF16)
-        for half in range(2):
-            slots = slice(half * SLOTS // 2, (half + 1) * SLOTS // 2)
+        x_halves = [slice(0, SLOTS // 2), slice(SLOTS // 2, SLOTS)]
+        for slots in x_halves:
             nc.sync.dma_start(out=x_sb[:, slots, :], in_=x_rows[:, slots, :])
         a_sb = consts.tile([P, SLOTS * K], BF16)
         for g in groups:
@@ -100,19 +100,14 @@ def tile_windowattentionblock_pb_s_kernel(tc, attn_ctx, x, wo, bo, out):
 
         x_plus_bo = consts.tile([P, SLOTS, C], F32)
 
-        def add_bias_to_x(g):
+        for slots in x_halves:
             nc.vector.tensor_tensor(
-                out=x_plus_bo[:, slots_of(g), :],
-                in0=x_sb[:, slots_of(g), :],
-                in1=bo_all[:].unsqueeze(1).to_broadcast([P, PAIR, C]),
+                out=x_plus_bo[:, slots, :],
+                in0=x_sb[:, slots, :],
+                in1=bo_all[:].unsqueeze(1).to_broadcast([P, SLOTS // 2, C]),
                 op=ADD,
             )
-
-        add_bias_to_x(0)
-        add_bias_to_x(1)
         quantise_wo()
-        add_bias_to_x(2)
-        add_bias_to_x(3)
 
         a_words = a_sb[:].bitcast(F32)
         words = K // 2

@@ -16,7 +16,6 @@ PACK = 4
 HALVES = 2
 C = 256
 SLOTS = 8
-PAIR = 2
 SHIFT = 4
 
 FLOPS = 2 * 1024 * K * C
@@ -43,12 +42,12 @@ def build_permutations(nc, consts):
 
 def tile_windowattentionblock_pb_s_kernel(tc, attn_ctx, x, wo, bo, out):
     nc = tc.nc
-    groups = range(SLOTS // PAIR)
+    groups = [(0, 1), (1, 1), (2, 2), (4, 2), (6, 2)]
     with ExitStack() as stack:
         consts = stack.enter_context(tc.tile_pool(name="consts", bufs=1))
         work = stack.enter_context(tc.tile_pool(name="work", bufs=len(groups)))
         psum_bias = stack.enter_context(tc.psum_pool(name="psum_bias", bufs=1))
-        psum_t = stack.enter_context(tc.psum_pool(name="psum_t", bufs=len(groups)))
+        psum_t = stack.enter_context(tc.psum_pool(name="psum_t", bufs=4))
         psum_acc = stack.enter_context(tc.psum_pool(name="psum_acc", bufs=3))
         stack.enter_context(tc.manual_schedule())
 
@@ -60,86 +59,123 @@ def tile_windowattentionblock_pb_s_kernel(tc, attn_ctx, x, wo, bo, out):
         )
 
         def slots_of(g):
-            return slice(g * PAIR, (g + 1) * PAIR)
+            first, count = groups[g]
+            return slice(first, first + count)
 
         def first_tj(g):
-            return (g * PAIR + SHIFT) % SLOTS
+            return (groups[g][0] + SHIFT) % SLOTS
 
-        bo_row0 = consts.tile([P, C], BF16)
-        nc.vector.memset(bo_row0[:], 0.0)
-        w_raw = consts.tile([P, PACK, C], BF16)
-        nc.sync.dma_start(out=w_raw[:].rearrange("p (u e) c -> p u (e c)", u=HALVES), in_=wo_rows)
-        nc.sync.dma_start(out=bo_row0[0:1, :], in_=bo.rearrange("(o c) -> o c", o=1))
         x_sb = consts.tile([P, SLOTS, C], BF16)
-        x_halves = [slice(0, SLOTS // 2), slice(SLOTS // 2, SLOTS)]
-        for slots in x_halves:
-            nc.sync.dma_start(out=x_sb[:, slots, :], in_=x_rows[:, slots, :])
         a_sb = consts.tile([P, SLOTS * K], BF16)
-        for g in groups:
-            columns = slice(first_tj(g) * K, (first_tj(g) + PAIR) * K)
+        w_raw = consts.tile([P, PACK, C], BF16)
+        bo_row0 = consts.tile([P, C], BF16)
+        low, high = slice(0, SLOTS // 2), slice(SLOTS // 2, SLOTS)
+
+        def load_x(slots):
+            nc.sync.dma_start(out=x_sb[:, slots, :], in_=x_rows[:, slots, :])
+
+        def load_tokens(g):
+            columns = slice(first_tj(g) * K, (first_tj(g) + groups[g][1]) * K)
             nc.sync.dma_start(out=a_sb[:, columns], in_=attn_rows[:, columns])
 
+        load_x(low)
+        nc.vector.memset(bo_row0[:], 0.0)
+        nc.sync.dma_start(out=bo_row0[0:1, :], in_=bo.rearrange("(o c) -> o c", o=1))
+        load_x(high)
+        nc.sync.dma_start(out=w_raw[:].rearrange("p (u e) c -> p u (e c)", u=HALVES), in_=wo_rows)
+        load_tokens(0)
+        load_tokens(1)
+        load_tokens(2)
+        load_tokens(3)
+        load_tokens(4)
+
+        zeros = consts.tile([P, P], F32)
+        nc.vector.memset(zeros[:], 0.0)
         ones = consts.tile([P, P], BF16)
         nc.vector.memset(ones[:], 1.0)
         perm_stay, perm_next = build_permutations(nc, consts)
 
+        idle_work = psum_t.tile([P, 2, HALVES, P], F32, name="transposed")
+
+        def keep_busy(times):
+            for s in range(times):
+                nc.tensor.matmul(
+                    out=idle_work[:, 0, 0, :], lhsT=zeros[:], rhs=zeros[:], start=True, stop=True
+                )
+
+        keep_busy(2)
         bo_all = psum_bias.tile([P, C], F32)
         nc.tensor.matmul(out=bo_all[:], lhsT=ones[:], rhs=bo_row0[:], start=True, stop=True)
+        keep_busy(2)
 
         w_grouped = consts.tile([P, C, PACK], BF16, align_bytes=64)
-        nc.scalar.copy(out=w_grouped[:], in_=w_raw[:].rearrange("p t c -> p c t"))
+        nc.gpsimd.tensor_scalar(
+            out=w_grouped[:],
+            in0=w_raw[:].rearrange("p t c -> p c t"),
+            scalar1=1.0,
+            scalar2=0.0,
+            op0=mybir.AluOpType.mult,
+            op1=ADD,
+        )
         w_codes = consts.tile([P, C], U32, align_bytes=64)
         w_scales = consts.tile([P, C], U8, align_bytes=64)
 
-        def quantise_wo():
-            nc.vector.quantize_mx(
-                out=w_codes[:].bitcast(FP8X4),
-                scales=w_scales[:],
-                in_=w_grouped[:].rearrange("p c t -> p (c t)"),
-            )
-
         x_plus_bo = consts.tile([P, SLOTS, C], F32)
-
-        for slots in x_halves:
+        for slots in (low, high):
             nc.vector.tensor_tensor(
                 out=x_plus_bo[:, slots, :],
                 in0=x_sb[:, slots, :],
                 in1=bo_all[:].unsqueeze(1).to_broadcast([P, SLOTS // 2, C]),
                 op=ADD,
             )
-        quantise_wo()
+
+        nc.vector.quantize_mx(
+            out=w_codes[:].bitcast(FP8X4),
+            scales=w_scales[:],
+            in_=w_grouped[:].rearrange("p c t -> p (c t)"),
+        )
 
         a_words = a_sb[:].bitcast(F32)
         words = K // 2
         grouped = []
-        for g in groups:
+
+        def turn(g):
+            count = groups[g][1]
             perm = perm_stay if first_tj(g) < SHIFT else perm_next
-            transposed = psum_t.tile([P, PAIR, HALVES, P], F32)
-            for s in range(PAIR):
+            transposed = psum_t.tile([P, count, HALVES, P], F32)
+            for s in range(count):
                 for u in range(HALVES):
                     first = (first_tj(g) + s) * words + u * P
                     nc.tensor.transpose(
                         transposed[:, s, u, :], a_words[:, first : first + P], perm[:]
                     )
-            side_by_side = work.tile([P, PAIR * P * PACK], BF16, align_bytes=64)
+            side_by_side = work.tile([P, count * P * PACK], BF16, align_bytes=64)
             nc.scalar.copy(
                 out=side_by_side[:]
                 .bitcast(F32)
-                .rearrange("p (s q u) -> p s q u", s=PAIR, u=HALVES),
+                .rearrange("p (s q u) -> p s q u", s=count, u=HALVES),
                 in_=transposed[:].rearrange("p s u q -> p s q u"),
             )
             grouped.append(side_by_side)
 
-        sums = []
+        codes = []
 
-        def project(g):
-            a_codes = work.tile([P, PAIR * P], U32, align_bytes=64)
-            a_scales = work.tile([P, PAIR * P], U8, align_bytes=64)
+        def quantise(g):
+            width = groups[g][1] * P
+            a_codes = work.tile([P, width], U32, align_bytes=64)
+            a_scales = work.tile([P, width], U8, align_bytes=64)
             nc.vector.quantize_mx(
                 out=a_codes[:].bitcast(FP8X4), scales=a_scales[:], in_=grouped[g][:]
             )
-            acc = psum_acc.tile([P, PAIR, C], F32)
-            for s in range(PAIR):
+            codes.append((a_codes, a_scales))
+
+        sums = []
+
+        def multiply(g):
+            count = groups[g][1]
+            a_codes, a_scales = codes[g]
+            acc = psum_acc.tile([P, count, C], F32)
+            for s in range(count):
                 pixels = slice(s * P, (s + 1) * P)
                 nc.tensor.matmul_mx(
                     out=acc[:, s, :],
@@ -153,14 +189,29 @@ def tile_windowattentionblock_pb_s_kernel(tc, attn_ctx, x, wo, bo, out):
             sums.append(acc)
 
         def finish(g):
-            result = work.tile([P, PAIR, C], F32)
+            result = work.tile([P, groups[g][1], C], F32)
             nc.vector.tensor_tensor(
                 out=result[:], in0=sums[g][:], in1=x_plus_bo[:, slots_of(g), :], op=ADD
             )
             nc.sync.dma_start(out=out_rows[:, slots_of(g), :], in_=result[:])
 
-        project(0)
-        for g in groups[1:]:
-            project(g)
-            finish(g - 1)
-        finish(groups[-1])
+        turn(0)
+        turn(1)
+        turn(2)
+        turn(3)
+        quantise(0)
+        multiply(0)
+        quantise(1)
+        multiply(1)
+        turn(4)
+        quantise(2)
+        multiply(2)
+        finish(0)
+        finish(1)
+        quantise(3)
+        multiply(3)
+        finish(2)
+        quantise(4)
+        multiply(4)
+        finish(3)
+        finish(4)

@@ -37,7 +37,7 @@ def build_permutations(nc, consts):
     moved = perm_next[:].rearrange("p (i jb) -> p i jb", jb=4)
     nc.vector.tensor_copy(out=moved[:, :, 1:4], in_=stay[:, :, 0:3])
     nc.vector.tensor_copy(out=moved[:, :, 0:1], in_=stay[:, :, 3:4])
-    return perm_stay, perm_next
+    return ident, perm_stay, perm_next
 
 
 def tile_windowattentionblock_pb_s_kernel(tc, attn_ctx, x, wo, bo, out):
@@ -47,7 +47,7 @@ def tile_windowattentionblock_pb_s_kernel(tc, attn_ctx, x, wo, bo, out):
         consts = stack.enter_context(tc.tile_pool(name="consts", bufs=1))
         work = stack.enter_context(tc.tile_pool(name="work", bufs=len(groups)))
         psum_bias = stack.enter_context(tc.psum_pool(name="psum_bias", bufs=1))
-        psum_t = stack.enter_context(tc.psum_pool(name="psum_t", bufs=4))
+        psum_t = stack.enter_context(tc.psum_pool(name="psum_t", bufs=3))
         psum_acc = stack.enter_context(tc.psum_pool(name="psum_acc", bufs=3))
         stack.enter_context(tc.manual_schedule())
 
@@ -68,7 +68,7 @@ def tile_windowattentionblock_pb_s_kernel(tc, attn_ctx, x, wo, bo, out):
         x_sb = consts.tile([P, SLOTS, C], BF16)
         a_sb = consts.tile([P, SLOTS * K], BF16)
         w_raw = consts.tile([P, PACK, C], BF16)
-        bo_row0 = consts.tile([P, C], BF16)
+        bo_pairs = consts.tile([P, 2], BF16)
         low, high = slice(0, SLOTS // 2), slice(SLOTS // 2, SLOTS)
 
         def load_x(slots):
@@ -78,9 +78,9 @@ def tile_windowattentionblock_pb_s_kernel(tc, attn_ctx, x, wo, bo, out):
             columns = slice(first_tj(g) * K, (first_tj(g) + groups[g][1]) * K)
             nc.sync.dma_start(out=a_sb[:, columns], in_=attn_rows[:, columns])
 
+        nc.scalar.dma_start(out=bo_pairs[:], in_=bo.rearrange("(p e) -> p e", e=2))
+
         load_x(low)
-        nc.vector.memset(bo_row0[:], 0.0)
-        nc.sync.dma_start(out=bo_row0[0:1, :], in_=bo.rearrange("(o c) -> o c", o=1))
         load_x(high)
         nc.sync.dma_start(out=w_raw[:].rearrange("p (u e) c -> p u (e c)", u=HALVES), in_=wo_rows)
         load_tokens(0)
@@ -91,22 +91,25 @@ def tile_windowattentionblock_pb_s_kernel(tc, attn_ctx, x, wo, bo, out):
 
         zeros = consts.tile([P, P], F32)
         nc.vector.memset(zeros[:], 0.0)
-        ones = consts.tile([P, P], BF16)
-        nc.vector.memset(ones[:], 1.0)
-        perm_stay, perm_next = build_permutations(nc, consts)
+        ident, perm_stay, perm_next = build_permutations(nc, consts)
 
-        idle_work = psum_t.tile([P, 2, HALVES, P], F32, name="transposed")
+        idle_work = psum_bias.tile([P, P], F32)
 
-        def keep_busy(times):
-            for s in range(times):
-                nc.tensor.matmul(
-                    out=idle_work[:, 0, 0, :], lhsT=zeros[:], rhs=zeros[:], start=True, stop=True
-                )
+        def keep_busy(words):
+            nc.tensor.matmul(
+                out=idle_work[:], lhsT=zeros[:], rhs=words[:, 0:P], start=True, stop=True
+            )
 
-        keep_busy(2)
-        bo_all = psum_bias.tile([P, C], F32)
-        nc.tensor.matmul(out=bo_all[:], lhsT=ones[:], rhs=bo_row0[:], start=True, stop=True)
-        keep_busy(2)
+        keep_busy(zeros)
+        keep_busy(zeros)
+
+        bo_words = psum_bias.tile([P, P], F32)
+        nc.tensor.transpose(
+            bo_words[:], bo_pairs[:].bitcast(F32).to_broadcast([P, P]), ident[:]
+        )
+        bo_all = bo_words[:].bitcast(BF16)
+        keep_busy(x_sb[:, SLOTS // 2, :].bitcast(F32))
+        keep_busy(w_raw[:, 0, :].bitcast(F32))
 
         w_grouped = consts.tile([P, C, PACK], BF16, align_bytes=64)
         nc.gpsimd.tensor_scalar(
@@ -125,7 +128,7 @@ def tile_windowattentionblock_pb_s_kernel(tc, attn_ctx, x, wo, bo, out):
             nc.vector.tensor_tensor(
                 out=x_plus_bo[:, slots, :],
                 in0=x_sb[:, slots, :],
-                in1=bo_all[:].unsqueeze(1).to_broadcast([P, SLOTS // 2, C]),
+                in1=bo_all.unsqueeze(1).to_broadcast([P, SLOTS // 2, C]),
                 op=ADD,
             )
 
@@ -198,7 +201,9 @@ def tile_windowattentionblock_pb_s_kernel(tc, attn_ctx, x, wo, bo, out):
         turn(0)
         turn(1)
         turn(2)
+        keep_busy(zeros)
         turn(3)
+        keep_busy(zeros)
         quantise(0)
         multiply(0)
         quantise(1)

@@ -42,7 +42,7 @@ def build_permutations(nc, consts):
 
 def tile_windowattentionblock_pb_s_kernel(tc, attn_ctx, x, wo, bo, out):
     nc = tc.nc
-    groups = [(0, 1), (1, 1), (2, 2), (4, 2), (6, 2)]
+    groups = [(0, 1), (1, 1), (2, 2), (4, 2), (6, 1), (7, 1)]
     with ExitStack() as stack:
         consts = stack.enter_context(tc.tile_pool(name="consts", bufs=1))
         work = stack.enter_context(tc.tile_pool(name="work", bufs=len(groups)))
@@ -74,20 +74,19 @@ def tile_windowattentionblock_pb_s_kernel(tc, attn_ctx, x, wo, bo, out):
         def load_x(slots):
             nc.sync.dma_start(out=x_sb[:, slots, :], in_=x_rows[:, slots, :])
 
-        def load_tokens(g):
-            columns = slice(first_tj(g) * K, (first_tj(g) + groups[g][1]) * K)
+        def load_tokens(first, last):
+            columns = slice(first_tj(first) * K, (first_tj(last) + groups[last][1]) * K)
             nc.sync.dma_start(out=a_sb[:, columns], in_=attn_rows[:, columns])
 
-        nc.scalar.dma_start(out=bo_pairs[:], in_=bo.rearrange("(p e) -> p e", e=2))
-
+        nc.sync.dma_start(out=bo_pairs[:], in_=bo.rearrange("(p e) -> p e", e=2))
         load_x(low)
-        load_x(high)
         nc.sync.dma_start(out=w_raw[:].rearrange("p (u e) c -> p u (e c)", u=HALVES), in_=wo_rows)
-        load_tokens(0)
-        load_tokens(1)
-        load_tokens(2)
-        load_tokens(3)
-        load_tokens(4)
+        load_x(high)
+        load_tokens(0, 0)
+        load_tokens(1, 1)
+        load_tokens(2, 2)
+        load_tokens(3, 3)
+        load_tokens(4, 5)
 
         zeros = consts.tile([P, P], F32)
         nc.vector.memset(zeros[:], 0.0)
@@ -102,14 +101,15 @@ def tile_windowattentionblock_pb_s_kernel(tc, attn_ctx, x, wo, bo, out):
 
         keep_busy(zeros)
         keep_busy(zeros)
+        keep_busy(zeros)
 
         bo_words = psum_bias.tile([P, P], F32)
         nc.tensor.transpose(
             bo_words[:], bo_pairs[:].bitcast(F32).to_broadcast([P, P]), ident[:]
         )
         bo_all = bo_words[:].bitcast(BF16)
-        keep_busy(x_sb[:, SLOTS // 2, :].bitcast(F32))
         keep_busy(w_raw[:, 0, :].bitcast(F32))
+        keep_busy(x_sb[:, SLOTS // 2, :].bitcast(F32))
 
         w_grouped = consts.tile([P, C, PACK], BF16, align_bytes=64)
         nc.gpsimd.tensor_scalar(
@@ -124,14 +124,18 @@ def tile_windowattentionblock_pb_s_kernel(tc, attn_ctx, x, wo, bo, out):
         w_scales = consts.tile([P, C], U8, align_bytes=64)
 
         x_plus_bo = consts.tile([P, SLOTS, C], F32)
-        for slots in (low, high):
+
+        def add_bias(first, count):
+            slots = slice(first, first + count)
             nc.vector.tensor_tensor(
                 out=x_plus_bo[:, slots, :],
                 in0=x_sb[:, slots, :],
-                in1=bo_all.unsqueeze(1).to_broadcast([P, SLOTS // 2, C]),
+                in1=bo_all.unsqueeze(1).to_broadcast([P, count, C]),
                 op=ADD,
             )
 
+        add_bias(0, 4)
+        add_bias(4, 4)
         nc.vector.quantize_mx(
             out=w_codes[:].bitcast(FP8X4),
             scales=w_scales[:],
@@ -203,12 +207,12 @@ def tile_windowattentionblock_pb_s_kernel(tc, attn_ctx, x, wo, bo, out):
         turn(2)
         keep_busy(zeros)
         turn(3)
-        keep_busy(zeros)
         quantise(0)
         multiply(0)
         quantise(1)
         multiply(1)
         turn(4)
+        turn(5)
         quantise(2)
         multiply(2)
         finish(0)
@@ -218,5 +222,8 @@ def tile_windowattentionblock_pb_s_kernel(tc, attn_ctx, x, wo, bo, out):
         finish(2)
         quantise(4)
         multiply(4)
+        quantise(5)
+        multiply(5)
         finish(3)
         finish(4)
+        finish(5)

@@ -69,7 +69,7 @@ def tile_windowattentionblock_pb_s_kernel(tc, attn_ctx, x, wo, bo, out):
         a_sb = consts.tile([P, SLOTS * K], BF16)
         w_raw = consts.tile([P, PACK, C], BF16)
         bo_pairs = consts.tile([P, 2], BF16)
-        low, high = slice(0, SLOTS // 2), slice(SLOTS // 2, SLOTS)
+        low, middle, high = slice(0, 4), slice(4, 6), slice(6, 8)
 
         def load_x(slots):
             nc.sync.dma_start(out=x_sb[:, slots, :], in_=x_rows[:, slots, :])
@@ -81,10 +81,11 @@ def tile_windowattentionblock_pb_s_kernel(tc, attn_ctx, x, wo, bo, out):
         nc.sync.dma_start(out=bo_pairs[:], in_=bo.rearrange("(p e) -> p e", e=2))
         load_x(low)
         nc.sync.dma_start(out=w_raw[:].rearrange("p (u e) c -> p u (e c)", u=HALVES), in_=wo_rows)
-        load_x(high)
+        load_x(middle)
         load_tokens(0, 0)
         load_tokens(1, 1)
         load_tokens(2, 2)
+        load_x(high)
         load_tokens(3, 3)
         load_tokens(4, 5)
 
@@ -135,7 +136,7 @@ def tile_windowattentionblock_pb_s_kernel(tc, attn_ctx, x, wo, bo, out):
             )
 
         add_bias(0, 4)
-        add_bias(4, 4)
+        add_bias(4, 2)
         nc.vector.quantize_mx(
             out=w_codes[:].bitcast(FP8X4),
             scales=w_scales[:],
@@ -213,6 +214,7 @@ def tile_windowattentionblock_pb_s_kernel(tc, attn_ctx, x, wo, bo, out):
         multiply(1)
         turn(4)
         turn(5)
+        add_bias(6, 2)
         quantise(2)
         multiply(2)
         finish(0)

@@ -113,14 +113,7 @@ def tile_windowattentionblock_pb_s_kernel(tc, attn_ctx, x, wo, bo, out):
         keep_busy(x_sb[:, SLOTS // 2, :].bitcast(F32))
 
         w_grouped = consts.tile([P, C, PACK], BF16, align_bytes=64)
-        nc.gpsimd.tensor_scalar(
-            out=w_grouped[:],
-            in0=w_raw[:].rearrange("p t c -> p c t"),
-            scalar1=1.0,
-            scalar2=0.0,
-            op0=mybir.AluOpType.mult,
-            op1=ADD,
-        )
+        nc.scalar.copy(out=w_grouped[:], in_=w_raw[:].rearrange("p t c -> p c t"))
         w_codes = consts.tile([P, C], U32, align_bytes=64)
         w_scales = consts.tile([P, C], U8, align_bytes=64)
 
@@ -196,12 +189,18 @@ def tile_windowattentionblock_pb_s_kernel(tc, attn_ctx, x, wo, bo, out):
                 )
             sums.append(acc)
 
+        results = consts.tile([P, SLOTS, C], F32)
+
         def finish(g):
-            result = work.tile([P, groups[g][1], C], F32)
             nc.vector.tensor_tensor(
-                out=result[:], in0=sums[g][:], in1=x_plus_bo[:, slots_of(g), :], op=ADD
+                out=results[:, slots_of(g), :],
+                in0=sums[g][:],
+                in1=x_plus_bo[:, slots_of(g), :],
+                op=ADD,
             )
-            nc.sync.dma_start(out=out_rows[:, slots_of(g), :], in_=result[:])
+
+        def store(slots):
+            nc.sync.dma_start(out=out_rows[:, slots, :], in_=results[:, slots, :])
 
         turn(0)
         turn(1)
@@ -219,13 +218,15 @@ def tile_windowattentionblock_pb_s_kernel(tc, attn_ctx, x, wo, bo, out):
         multiply(2)
         finish(0)
         finish(1)
+        store(slice(0, 2))
         quantise(3)
         multiply(3)
         finish(2)
+        store(slots_of(2))
         quantise(4)
         multiply(4)
         quantise(5)
         multiply(5)
-        finish(3)
-        finish(4)
-        finish(5)
+        for g in (3, 4, 5):
+            finish(g)
+            store(slots_of(g))

from contextlib import ExitStack

import concourse.mybir as mybir
from concourse.masks import make_identity

F32 = mybir.dt.float32
BF16 = mybir.dt.bfloat16
U32 = mybir.dt.uint32
U8 = mybir.dt.uint8
FP8X4 = mybir.dt.float8_e4m3fn_x4
ADD = mybir.AluOpType.add

P = 128
K = 512
PACK = 4
HALVES = 2
C = 256
SLOTS = 8
SHIFT = 4

FLOPS = 2 * 1024 * K * C


def build_permutations(nc, consts):
    ident = consts.tile([P, P], F32)
    make_identity(nc, ident[:])
    perm_stay = consts.tile([P, P], F32)
    perm_next = consts.tile([P, P], F32)

    by_token = ident[:].rearrange("p (gi gj th tl) -> p gi th tl gj", gi=4, gj=4, th=2, tl=4)
    by_pixel = perm_stay[:].rearrange("p (rh rl tl jb) -> p rh rl tl jb", rh=4, rl=2, tl=4, jb=4)
    nc.vector.tensor_copy(out=by_pixel[:, :, 1], in_=by_token[:, :, 0])
    nc.vector.tensor_copy(out=by_pixel[:, 1:4, 0], in_=by_token[:, 0:3, 1])
    nc.vector.tensor_copy(out=by_pixel[:, 0:1, 0], in_=by_token[:, 3:4, 1])

    stay = perm_stay[:].rearrange("p (i jb) -> p i jb", jb=4)
    moved = perm_next[:].rearrange("p (i jb) -> p i jb", jb=4)
    nc.vector.tensor_copy(out=moved[:, :, 1:4], in_=stay[:, :, 0:3])
    nc.vector.tensor_copy(out=moved[:, :, 0:1], in_=stay[:, :, 3:4])
    return ident, perm_stay, perm_next


def tile_windowattentionblock_pb_s_kernel(tc, attn_ctx, x, wo, bo, out):
    nc = tc.nc
    groups = [(0, 1), (1, 1), (2, 2), (4, 2), (6, 1), (7, 1)]
    with ExitStack() as stack:
        consts = stack.enter_context(tc.tile_pool(name="consts", bufs=1))
        work = stack.enter_context(tc.tile_pool(name="work", bufs=len(groups)))
        psum_bias = stack.enter_context(tc.psum_pool(name="psum_bias", bufs=1))
        psum_t = stack.enter_context(tc.psum_pool(name="psum_t", bufs=3))
        psum_acc = stack.enter_context(tc.psum_pool(name="psum_acc", bufs=3))
        stack.enter_context(tc.manual_schedule())

        attn_rows = attn_ctx.rearrange("n (ti tj) h d -> (n ti) (tj h d)", tj=SLOTS)
        x_rows = x.rearrange("b i (jb s) c -> (b i jb) s c", s=SLOTS)
        out_rows = out.rearrange("b i (jb s) c -> (b i jb) s c", s=SLOTS)
        wo_rows = wo.rearrange("h d c -> (h d) c").rearrange(
            "(u p e) c -> p u (e c)", u=HALVES, p=P
        )

        def slots_of(g):
            first, count = groups[g]
            return slice(first, first + count)

        def first_tj(g):
            return (groups[g][0] + SHIFT) % SLOTS

        x_sb = consts.tile([P, SLOTS, C], BF16)
        a_sb = consts.tile([P, SLOTS * K], BF16)
        w_raw = consts.tile([P, PACK, C], BF16)
        bo_pairs = consts.tile([P, 2], BF16)
        low, middle, high = slice(0, 4), slice(4, 6), slice(6, 8)

        def load_x(slots):
            nc.sync.dma_start(out=x_sb[:, slots, :], in_=x_rows[:, slots, :])

        def load_tokens(first, last):
            columns = slice(first_tj(first) * K, (first_tj(last) + groups[last][1]) * K)
            nc.sync.dma_start(out=a_sb[:, columns], in_=attn_rows[:, columns])

        nc.sync.dma_start(out=bo_pairs[:], in_=bo.rearrange("(p e) -> p e", e=2))
        load_x(low)
        nc.sync.dma_start(out=w_raw[:].rearrange("p (u e) c -> p u (e c)", u=HALVES), in_=wo_rows)
        load_x(middle)
        load_tokens(0, 0)
        load_tokens(1, 1)
        load_tokens(2, 2)
        load_x(high)
        load_tokens(3, 3)
        load_tokens(4, 5)

        zeros = consts.tile([P, P], F32)
        nc.vector.memset(zeros[:], 0.0)
        ident, perm_stay, perm_next = build_permutations(nc, consts)

        idle_work = psum_bias.tile([P, P], F32)

        def keep_busy(words):
            nc.tensor.matmul(
                out=idle_work[:], lhsT=zeros[:], rhs=words[:, 0:P], start=True, stop=True
            )

        keep_busy(zeros)
        keep_busy(zeros)
        keep_busy(zeros)

        bo_words = psum_bias.tile([P, P], F32)
        nc.tensor.transpose(
            bo_words[:], bo_pairs[:].bitcast(F32).to_broadcast([P, P]), ident[:]
        )
        bo_all = bo_words[:].bitcast(BF16)
        keep_busy(w_raw[:, 0, :].bitcast(F32))
        keep_busy(x_sb[:, SLOTS // 2, :].bitcast(F32))

        w_grouped = consts.tile([P, C, PACK], BF16, align_bytes=64)
        nc.scalar.copy(out=w_grouped[:], in_=w_raw[:].rearrange("p t c -> p c t"))
        w_codes = consts.tile([P, C], U32, align_bytes=64)
        w_scales = consts.tile([P, C], U8, align_bytes=64)

        x_plus_bo = consts.tile([P, SLOTS, C], F32)

        def add_bias(first, count):
            slots = slice(first, first + count)
            nc.vector.tensor_tensor(
                out=x_plus_bo[:, slots, :],
                in0=x_sb[:, slots, :],
                in1=bo_all.unsqueeze(1).to_broadcast([P, count, C]),
                op=ADD,
            )

        add_bias(0, 4)
        add_bias(4, 2)
        nc.vector.quantize_mx(
            out=w_codes[:].bitcast(FP8X4),
            scales=w_scales[:],
            in_=w_grouped[:].rearrange("p c t -> p (c t)"),
        )

        a_words = a_sb[:].bitcast(F32)
        words = K // 2
        grouped = []

        def turn(g):
            count = groups[g][1]
            perm = perm_stay if first_tj(g) < SHIFT else perm_next
            transposed = psum_t.tile([P, count, HALVES, P], F32)
            for s in range(count):
                for u in range(HALVES):
                    first = (first_tj(g) + s) * words + u * P
                    nc.tensor.transpose(
                        transposed[:, s, u, :], a_words[:, first : first + P], perm[:]
                    )
            side_by_side = work.tile([P, count * P * PACK], BF16, align_bytes=64)
            nc.scalar.copy(
                out=side_by_side[:]
                .bitcast(F32)
                .rearrange("p (s q u) -> p s q u", s=count, u=HALVES),
                in_=transposed[:].rearrange("p s u q -> p s q u"),
            )
            grouped.append(side_by_side)

        codes = []

        def quantise(g):
            width = groups[g][1] * P
            a_codes = work.tile([P, width], U32, align_bytes=64)
            a_scales = work.tile([P, width], U8, align_bytes=64)
            nc.vector.quantize_mx(
                out=a_codes[:].bitcast(FP8X4), scales=a_scales[:], in_=grouped[g][:]
            )
            codes.append((a_codes, a_scales))

        sums = []

        def multiply(g):
            count = groups[g][1]
            a_codes, a_scales = codes[g]
            acc = psum_acc.tile([P, count, C], F32)
            for s in range(count):
                pixels = slice(s * P, (s + 1) * P)
                nc.tensor.matmul_mx(
                    out=acc[:, s, :],
                    lhsT=a_codes[:, pixels].bitcast(FP8X4),
                    lhsT_scale=a_scales[:, pixels],
                    rhs=w_codes[:].bitcast(FP8X4),
                    rhs_scale=w_scales[:],
                    start=True,
                    stop=True,
                )
            sums.append(acc)

        results = consts.tile([P, SLOTS, C], F32)

        def finish(g):
            nc.vector.tensor_tensor(
                out=results[:, slots_of(g), :],
                in0=sums[g][:],
                in1=x_plus_bo[:, slots_of(g), :],
                op=ADD,
            )

        def store(slots):
            nc.sync.dma_start(out=out_rows[:, slots, :], in_=results[:, slots, :])

        turn(0)
        turn(1)
        turn(2)
        keep_busy(zeros)
        turn(3)
        quantise(0)
        multiply(0)
        quantise(1)
        multiply(1)
        turn(4)
        turn(5)
        add_bias(6, 2)
        quantise(2)
        multiply(2)
        finish(0)
        finish(1)
        store(slice(0, 2))
        quantise(3)
        multiply(3)
        finish(2)
        store(slots_of(2))
        quantise(4)
        multiply(4)
        quantise(5)
        multiply(5)
        for g in (3, 4, 5):
            finish(g)
            store(slots_of(g))
